import numpy as np
import ml_dtypes


def mxq(x, axis, fmt="e4m3"):
    dtype, down = {"e4m3": (ml_dtypes.float8_e4m3fn, 7), "e5m2": (ml_dtypes.float8_e5m2, 14)}[fmt]
    v = np.moveaxis(np.asarray(x, np.float32).astype(ml_dtypes.bfloat16).astype(np.float64), axis, -1)
    blocks = v.reshape(v.shape[:-1] + (-1, 32))
    amax = np.abs(blocks).max(-1, keepdims=True)
    byte = np.maximum(np.where(amax > 0, np.frexp(amax)[1] - 1 + 127, 0) - down, 1)
    scale = np.exp2(byte - 127.0)
    codes = (blocks / scale).astype(np.float32).astype(dtype).astype(np.float64)
    return np.moveaxis((codes * scale).reshape(v.shape), -1, axis)


WIDE = False


def mx_kscale(k):
    if not WIDE:
        return np.ones(k)
    levels = np.array([10, -10, 5, -5, 0])
    if k % 512:
        return np.exp2(np.random.permutation(np.resize(levels, k // 32))).repeat(32)
    a = np.empty((k // 512, 16))
    for p in range(k // 512):
        a[p, :8] = np.random.permutation(np.resize(levels, 8))
        for g in range(8):
            far = levels[np.abs(levels - a[p, g]) >= 10]
            a[p, g + 8] = far[np.random.randint(len(far))]
    return np.exp2(a.ravel()).repeat(32)


BF16 = ml_dtypes.bfloat16


def bf(x):
    return np.asarray(x, np.float32).astype(BF16)


def f64(x):
    return np.asarray(x).astype(np.float64)


B, N1, N2, D, H, DH = 4, 384, 128, 1024, 8, 128
E = H * DH


def rope_tables(n, d):
    inv = 1.0 / (10000.0 ** (np.arange(0, d, 2) / d))
    ang = np.outer(np.arange(n), inv)
    return np.repeat(np.cos(ang), 2, axis=-1), np.repeat(np.sin(ang), 2, axis=-1)


def apply_rope(x, cos, sin):
    xr = x.reshape(x.shape[:-1] + (-1, 2))
    x_real, x_imag = xr[..., 0], xr[..., 1]
    x_rot = np.stack([-x_imag, x_real], axis=-1).reshape(x.shape)
    return x * cos[None, None] + x_rot * sin[None, None]


def split_heads(t):
    b, n, _ = t.shape
    return t.reshape(b, n, H, DH).transpose(0, 2, 1, 3)


def draw0():
    s1, s2 = mx_kscale(D), mx_kscale(D)
    cos1, sin1 = rope_tables(N1, DH)
    cos2, sin2 = rope_tables(N2, DH)

    def w(s):
        return bf(np.random.standard_normal((D, E)) * 1.4 / np.sqrt(D) / s[:, None])

    def b():
        return bf(np.random.standard_normal(E) * 0.3)

    return {"x_1": bf(np.random.standard_normal((B, N1, D)) * s1), "x_2": bf(np.random.standard_normal((B, N2, D)) * s2),
            "cos1": bf(cos1), "sin1": bf(sin1), "cos2": bf(cos2), "sin2": bf(sin2),
            "wq1": w(s1), "bq1": b(), "wk1": w(s1), "bk1": b(),
            "wq2": w(s2), "bq2": b(), "wk2": w(s2), "bk2": b()}


def core(x_1, x_2, cos1, sin1, cos2, sin2, wq1, bq1, wk1, bk1, wq2, bq2, wk2, bk2):
    x1q = mxq(f64(x_1), 2, "e4m3")
    x2q = mxq(f64(x_2), 2, "e4m3")
    q = np.concatenate([(x1q @ mxq(f64(wq1), 0, "e4m3")) + f64(bq1),
                        (x2q @ mxq(f64(wq2), 0, "e4m3")) + f64(bq2)], axis=1)
    k = np.concatenate([(x1q @ mxq(f64(wk1), 0, "e4m3")) + f64(bk1),
                        (x2q @ mxq(f64(wk2), 0, "e4m3")) + f64(bk2)], axis=1)
    q, k = split_heads(q), split_heads(k)
    q = q * (DH ** -0.5)
    cos = np.concatenate([f64(cos1), f64(cos2)], axis=0)
    sin = np.concatenate([f64(sin1), f64(sin2)], axis=0)
    return apply_rope(q, cos, sin), apply_rope(k, cos, sin)


def e4m3fn_bytes(y):
    return np.clip(np.asarray(y, np.float64), -448.0, 448.0).astype(np.float32).astype(ml_dtypes.float8_e4m3fn).view(np.uint8)


def e4m3fn_values(b):
    return np.asarray(b, np.uint8).view(ml_dtypes.float8_e4m3fn).astype(np.float64)


def setup_inputs():
    d = draw0()
    x0 = np.asarray(d['x_1']).astype(np.float64)
    s = (np.max(np.abs(x0), axis=(0, 1), keepdims=True) / 448.0).astype(np.float32)
    out = {}
    for k, v in d.items():
        if k == 'x_1':
            out['x_1_bytes'] = e4m3fn_bytes(x0 / s.astype(np.float64))
            out['x_1_scale'] = s
        else:
            out[k] = v
    return out


def reference(x_1_bytes, x_1_scale, x_2, cos1, sin1, cos2, sin2, wq1, bq1, wk1, bk1, wq2, bq2, wk2, bk2):
    return core(e4m3fn_values(x_1_bytes) * x_1_scale.astype(np.float64), x_2, cos1, sin1, cos2, sin2, wq1, bq1, wk1, bk1, wq2, bq2, wk2, bk2)

@@ -1,0 +1,304 @@
+from contextlib import ExitStack
+
+import concourse.mybir as mybir
+from concourse.masks import make_identity
+
+F32 = mybir.dt.float32
+BF16 = mybir.dt.bfloat16
+U32 = mybir.dt.uint32
+U8 = mybir.dt.uint8
+FP8 = mybir.dt.float8_e4m3fn
+FP8X4 = mybir.dt.float8_e4m3fn_x4
+ALU = mybir.AluOpType
+ACT = mybir.ActivationFunctionType
+
+B, N1, N2, D, H, DH = 4, 384, 128, 1024, 8, 128
+E = H * DH
+P = 128
+K_PASS = 512
+CHUNK = 512
+PAIR = 2 * DH
+FLOPS = 2 * B * (N1 + N2) * D * 2 * E
+Q_FACTOR = DH ** -0.5
+
+BLOCKS_1 = B * N1 // P
+X2_CHUNK = 3
+W_ORDER = (0, 2, 1, 3)
+BANK_OF_PRODUCT = (0, 1, 1, 0)
+PRODUCT_ORDER = (2, 3, 0, 1)
+AHEAD = 2
+BEHIND = 2
+PIECE_LEAD = 6
+X2_FIRST_SLOT = 3
+
+
+def tile_dualmultiheadattention_pa_kernel(
+    tc, x_1_bytes, x_1_scale, x_2, cos1, sin1, cos2, sin2,
+    wq1, bq1, wk1, bk1, wq2, bq2, wk2, bk2, out_0, out_1,
+):
+    nc = tc.nc
+    weights = (wq1, wk1, wq2, wk2)
+    biases = (bq1, bk1, bq2, bk2)
+    outs = (out_0, out_1, out_0, out_1)
+
+    with ExitStack() as ctx:
+        const = ctx.enter_context(tc.tile_pool(name="const", bufs=1))
+        head = ctx.enter_context(tc.tile_pool(name="head", bufs=1))
+        wrawp = ctx.enter_context(tc.tile_pool(name="wrawp", bufs=6))
+        wgp = ctx.enter_context(tc.tile_pool(name="wgp", bufs=3))
+        wcp = ctx.enter_context(tc.tile_pool(name="wcp", bufs=6))
+        xbp = ctx.enter_context(tc.tile_pool(name="xbp", bufs=4))
+        xgp = ctx.enter_context(tc.tile_pool(name="xgp", bufs=2))
+        xcp = ctx.enter_context(tc.tile_pool(name="xcp", bufs=1))
+        up = ctx.enter_context(tc.tile_pool(name="up", bufs=4))
+        op = ctx.enter_context(tc.tile_pool(name="op", bufs=2))
+        accp = ctx.enter_context(tc.psum_pool(name="accp", bufs=2))
+        tps = ctx.enter_context(tc.psum_pool(name="tps", bufs=4))
+        ctx.enter_context(tc.manual_schedule())
+
+        bias_rows = head.tile([P, PAIR], BF16, name="bias_rows")
+        nc.gpsimd.memset(bias_rows[:], 0.0)
+        scale_all = head.tile([P, D], F32, name="scale_all")
+        nc.sync.dma_start(out=scale_all[:], in_=x_1_scale.rearrange("a b k -> (a b k)").partition_broadcast(P))
+        x1_bytes_sb = {}
+
+        def load_x1(b):
+            held = head.tile([P, 3 * D], U8, name="x1_bytes_sb%d" % b, tag="x1_bytes_sb%d" % b)
+            nc.sync.dma_start(out=held[:], in_=x_1_bytes[b].rearrange("(p i) k -> p (i k)", i=3))
+            x1_bytes_sb[b] = held
+
+        w_raw = {}
+
+        def load_w(w):
+            for g in range(2):
+                rows = wrawp.tile([P, 4, E], BF16, name="w_raw", tag="w_raw")
+                nc.sync.dma_start(out=rows[:], in_=weights[w][K_PASS * g:K_PASS * (g + 1), :].rearrange("(p r) c -> p r c", r=4))
+                w_raw[(w, g)] = rows
+
+        load_x1(0)
+        cos_rows = head.tile([P, 4, DH], BF16, name="cos_rows")
+        sin_rows = head.tile([P, 4, DH], BF16, name="sin_rows")
+        nc.sync.dma_start(out=cos_rows[:, 0:3, :], in_=cos1.rearrange("(a q) c -> q a c", q=P))
+        nc.sync.dma_start(out=sin_rows[:, 0:3, :], in_=sin1.rearrange("(a q) c -> q a c", q=P))
+        nc.sync.dma_start(out=cos_rows[:, 3, :], in_=cos2)
+        nc.sync.dma_start(out=sin_rows[:, 3, :], in_=sin2)
+        for w in range(4):
+            nc.sync.dma_start(out=bias_rows[4 * w:4 * w + 4, :], in_=biases[w].rearrange("(hp x) -> hp x", x=PAIR))
+        for b in range(1, B):
+            load_x1(b)
+        load_w(W_ORDER[0])
+        x2_sb = head.tile([P, B, D], BF16, name="x2_sb")
+        nc.sync.dma_start(out=x2_sb[:], in_=x_2.rearrange("b p k -> p b k"))
+        load_w(W_ORDER[1])
+        load_w(W_ORDER[2])
+
+        ident_f = const.tile([P, P], F32, name="ident_f")
+        make_identity(nc, ident_f[:])
+        ident_b = const.tile([P, P], BF16, name="ident_b")
+        make_identity(nc, ident_b[:])
+
+        table_rows = head.tile([P, 4, 4, DH], BF16, name="table_rows")
+        bias_rows_f = head.tile([P, PAIR], F32, name="bias_rows_f")
+        bias_col = const.tile([P, 2, P], F32, name="bias_col")
+        tables = const.tile([P, 4, 6 * P + CHUNK], BF16, name="tables")
+
+        def constants():
+            for hh in range(2):
+                for (t, rows, parity, sign) in ((0, cos_rows, 0, 1.0), (1, sin_rows, 0, -1.0), (2, cos_rows, 1, 1.0), (3, sin_rows, 1, 1.0)):
+                    nc.vector.tensor_scalar(out=table_rows[:, t, :, hh * 64:(hh + 1) * 64], in0=rows[:, :, parity:DH:2],
+                                            scalar1=sign, scalar2=None, op0=ALU.mult)
+            nc.vector.tensor_copy(out=bias_rows_f[:], in_=bias_rows[:])
+            bias_ps = tps.tile([P, 2, P], F32, name="bias_ps", tag="tp")
+            for e in range(2):
+                nc.tensor.transpose(bias_ps[:, e, :], bias_rows_f[:, e:PAIR:2], ident_f[:])
+            nc.scalar.copy(out=bias_col[:], in_=bias_ps[:])
+
+        table_ps = {}
+
+        def table_turn(t):
+            ps = tps.tile([P, 2 * CHUNK], BF16, name="table_ps", tag="tp")
+            for a in range(3):
+                nc.tensor.transpose(ps[:, a * P:(a + 1) * P], table_rows[:, t, a, :], ident_b[:])
+            for r in range(4):
+                nc.tensor.transpose(ps[:, N1 + r * P:N1 + (r + 1) * P], table_rows[:, t, 3, :], ident_b[:])
+            table_ps[t] = ps
+
+        def table_leave(t, part):
+            ps = table_ps[t]
+            if part < 2:
+                nc.scalar.copy(out=tables[:, t, N1 * part:N1 * (part + 1)].rearrange("m (i p) -> m i p", i=3),
+                               in_=ps[:, 0:N1].rearrange("m (p i) -> m i p", i=3))
+            else:
+                nc.scalar.copy(out=tables[:, t, 2 * N1:2 * N1 + CHUNK], in_=ps[:, N1:N1 + CHUNK])
+
+        x_grouped = {}
+        x_codes = {}
+
+        def x_turn(chunk, place, x_bf16):
+            if chunk not in x_grouped:
+                grouped = xgp.tile([P, 2, 2 * CHUNK], F32, name="x_grouped", tag="x_grouped", align_bytes=64)
+                x_grouped[chunk] = grouped
+            words = x_bf16.bitcast(F32)
+            ps = tps.tile([P, 2, 2, P], F32, name="x_ps", tag="tp")
+            for g in range(2):
+                for u in range(2):
+                    nc.tensor.transpose(ps[:, g, u, :], words[:, 256 * g + u:256 * (g + 1):2], ident_f[:])
+            nc.scalar.copy(out=x_grouped[chunk][:, :, place * 256:(place + 1) * 256].rearrange("p g (r u) -> p g r u", u=2),
+                           in_=ps[:].rearrange("p g u r -> p g r u"))
+
+        def x_quantise(chunk):
+            codes = xcp.tile([P, 2, CHUNK], U32, name="x_codes%d" % chunk, tag="x_codes%d" % chunk, align_bytes=64)
+            scales = xcp.tile([P, 2, CHUNK], U8, name="x_scales%d" % chunk, tag="x_scales%d" % chunk, align_bytes=64)
+            nc.vector.quantize_mx(out=codes[:].rearrange("p g c -> p (g c)").bitcast(FP8X4), scales=scales[:].rearrange("p g c -> p (g c)"),
+                                  in_=x_grouped[chunk][:].rearrange("p g w -> p (g w)").bitcast(BF16))
+            x_codes[chunk] = (codes, scales)
+
+        def x1_block(blk):
+            b, i = blk // 3, blk % 3
+            x_bf16 = xbp.tile([P, D], BF16, name="x_bf16", tag="x_bf16", align_bytes=64)
+            nc.vector.tensor_tensor(out=x_bf16[:], in0=x1_bytes_sb[b][:, i * D:(i + 1) * D].bitcast(FP8), in1=scale_all[:], op=ALU.mult)
+            x_turn(blk // 4, blk % 4, x_bf16[:])
+
+        groups = [(w, hp) for w in W_ORDER for hp in range(H // 2)]
+        w_grouped = {}
+        w_codes = {}
+
+        def w_piece(j):
+            gi, g = j // 2, j % 2
+            w, hp = groups[gi]
+            if g == 0:
+                grouped = wgp.tile([P, 2, 4 * PAIR], BF16, name="w_grouped", tag="w_grouped", align_bytes=64)
+                w_grouped[gi] = grouped
+            nc.scalar.copy(out=w_grouped[gi][:, g, :].rearrange("p (e m r) -> p e m r", e=2, r=4),
+                           in_=w_raw[(w, g)][:, :, hp * PAIR:(hp + 1) * PAIR].rearrange("p r (m e) -> p e m r", e=2))
+
+        def w_quantise(gi):
+            codes = wcp.tile([P, 2, PAIR], U32, name="w_codes", tag="w_codes", align_bytes=64)
+            scales = wcp.tile([P, 2, PAIR], U8, name="w_scales", tag="w_scales", align_bytes=64)
+            nc.vector.quantize_mx(out=codes[:].rearrange("p g c -> p (g c)").bitcast(FP8X4), scales=scales[:].rearrange("p g c -> p (g c)"),
+                                  in_=w_grouped[gi][:].rearrange("p g c -> p (g c)"))
+            w_codes[gi] = (codes, scales)
+
+        def w_quantise_slot(gi):
+            return max(2 * gi - 3, gi) if gi > 0 else -3
+
+        for blk in range(BLOCKS_1):
+            x1_block(blk)
+            if blk == 1:
+                constants()
+            if blk >= 2:
+                table_leave((blk - 2) // 3, (blk - 2) % 3)
+            if blk in (6, 7):
+                w_piece(blk - 6)
+            if blk % 3 == 1:
+                table_turn(blk // 3)
+            if blk in (5, 9):
+                x_quantise((blk - 5) // 4)
+        table_leave(3, 1)
+        table_leave(3, 2)
+
+        units = [(gi, chunk) for gi in range(len(groups)) for chunk in ((X2_CHUNK,) if groups[gi][0] >= 2 else (0, 1, 2))]
+        last = len(units) - 1
+        banks = {}
+        products = {}
+        turned = {}
+        out_sb = {}
+
+        def passes(k, e):
+            gi, chunk = units[k]
+            wc, ws = w_codes[gi]
+            xc, xs = x_codes[chunk]
+            bank = accp.tile([P, CHUNK], F32, name="bank%d" % e, tag="bank%d" % e)
+            for g in range(2):
+                nc.tensor.matmul_mx(out=bank[:], lhsT=wc[:, g, e * P:(e + 1) * P].bitcast(FP8X4), lhsT_scale=ws[:, g, e * P:(e + 1) * P],
+                                    rhs=xc[:, g, :].bitcast(FP8X4), rhs_scale=xs[:, g, :], start=(g == 0), stop=(g == 1))
+            banks[(k, e)] = bank
+
+        def product(k, t):
+            gi, chunk = units[k]
+            w, hp = groups[gi]
+            e = BANK_OF_PRODUCT[t]
+            at = 6 * P if chunk == X2_CHUNK else P * chunk
+            u = up.tile([P, CHUNK], F32, name="product%d" % t, tag="product%d" % t)
+            nc.vector.scalar_tensor_tensor(out=u[:], in0=banks[(k, e)][:], scalar=bias_col[:, e, 4 * w + hp:4 * w + hp + 1],
+                                           in1=tables[:, t, at:at + CHUNK], op0=ALU.add, op1=ALU.mult)
+            products[(k, t)] = u
+
+        def add_odd(k):
+            nc.gpsimd.tensor_tensor(out=products[(k, 2)][:], in0=products[(k, 2)][:], in1=products[(k, 3)][:], op=ALU.add)
+
+        def turn(k, half):
+            ps = tps.tile([P, 2, 2, P], F32, name="turned", tag="tp")
+            for ib in range(2):
+                cols = slice((2 * half + ib) * P, (2 * half + ib + 1) * P)
+                for e in range(2):
+                    if e == 0 or k == last:
+                        nc.tensor.matmul(out=ps[:, e, ib, :], lhsT=products[(k, 2 * e)][:, cols], rhs=ident_f[:], is_transpose=True, start=True, stop=False)
+                        nc.tensor.matmul(out=ps[:, e, ib, :], lhsT=products[(k, 2 * e + 1)][:, cols], rhs=ident_f[:], is_transpose=True, start=False, stop=True)
+                    else:
+                        nc.tensor.transpose(ps[:, e, ib, :], products[(k, 2)][:, cols], ident_f[:])
+            turned[(k, half)] = ps
+
+        def leave(k, half):
+            gi, chunk = units[k]
+            w, hp = groups[gi]
+            factor = Q_FACTOR if w % 2 == 0 else 1.0
+            for ib in range(2):
+                blk = 2 * half + ib
+                if chunk == X2_CHUNK:
+                    b, i = 0, blk
+                    if blk == 0:
+                        o2 = op.tile([P, 2, B, DH], F32, name="out2_sb", tag="out2_sb", bufs=2)
+                        out_sb[b] = o2
+                else:
+                    b, i = (4 * chunk + blk) // 3, (4 * chunk + blk) % 3
+                    if i == 0:
+                        o1 = op.tile([P, 2, 3, DH], F32, name="out1_sb", tag="out1_sb", bufs=6)
+                        out_sb[b] = o1
+                nc.scalar.activation(out=out_sb[b][:, :, i, :].rearrange("p hh (j e) -> p hh j e", e=2),
+                                     in_=turned[(k, half)][:, :, ib, :].rearrange("p e (hh j) -> p hh j e", hh=2),
+                                     func=ACT.Copy, scale=factor)
+                if chunk != X2_CHUNK and i == 2:
+                    nc.sync.dma_start(out=outs[w][b, 2 * hp:2 * hp + 2, 0:N1, :].rearrange("hh (p i) c -> p hh (i c)", i=3),
+                                      in_=out_sb[b][:].rearrange("p hh i c -> p hh (i c)"))
+            if chunk == X2_CHUNK and half == 1:
+                for hh in range(2):
+                    nc.sync.dma_start(out=outs[w][:, 2 * hp + hh, N1:N1 + N2, :].rearrange("b p c -> p b c"), in_=out_sb[0][:, hh, :, :])
+
+        for n in range(-PIECE_LEAD, len(units) + BEHIND):
+            live = 0 <= n <= last
+            ahead = 0 <= n + AHEAD <= last
+            behind = 0 <= n - BEHIND <= last
+            if behind:
+                turn(n - BEHIND, 0)
+                turn(n - BEHIND, 1)
+            if 0 <= n - X2_FIRST_SLOT < B:
+                x_turn(X2_CHUNK, n - X2_FIRST_SLOT, x2_sb[:, n - X2_FIRST_SLOT, :])
+            if live:
+                product(n, PRODUCT_ORDER[0])
+            for gi in range(len(groups)):
+                if n == w_quantise_slot(gi):
+                    w_quantise(gi)
+            if n == w_quantise_slot(0):
+                x_quantise(2)
+            if n == X2_FIRST_SLOT + B:
+                x_quantise(X2_CHUNK)
+            if live:
+                product(n, PRODUCT_ORDER[1])
+                if n < last:
+                    add_odd(n)
+                product(n, PRODUCT_ORDER[2])
+            if ahead:
+                passes(n + AHEAD, 0)
+            if live:
+                product(n, PRODUCT_ORDER[3])
+            if ahead:
+                passes(n + AHEAD, 1)
+            if behind:
+                leave(n - BEHIND, 0)
+            if 2 <= n + PIECE_LEAD < 2 * len(groups):
+                w_piece(n + PIECE_LEAD)
+            if n == X2_FIRST_SLOT:
+                load_w(W_ORDER[3])
+            if behind:
+                leave(n - BEHIND, 1)

@@ -24,8 +24,6 @@ Q_FACTOR = DH ** -0.5
 BLOCKS_1 = B * N1 // P
 X2_CHUNK = 3
 W_ORDER = (0, 2, 1, 3)
-BANK_OF_PRODUCT = (0, 1, 1, 0)
-PRODUCT_ORDER = (2, 3, 0, 1)
 AHEAD = 2
 BEHIND = 2
 PIECE_LEAD = 6
@@ -76,12 +74,13 @@ def tile_dualmultiheadattention_pa_kernel(
                 w_raw[(w, g)] = rows
 
         load_x1(0)
-        cos_rows = head.tile([P, 4, DH], BF16, name="cos_rows")
-        sin_rows = head.tile([P, 4, DH], BF16, name="sin_rows")
-        nc.sync.dma_start(out=cos_rows[:, 0:3, :], in_=cos1.rearrange("(a q) c -> q a c", q=P))
-        nc.sync.dma_start(out=sin_rows[:, 0:3, :], in_=sin1.rearrange("(a q) c -> q a c", q=P))
-        nc.sync.dma_start(out=cos_rows[:, 3, :], in_=cos2)
-        nc.sync.dma_start(out=sin_rows[:, 3, :], in_=sin2)
+        cos_rows = head.tile([P, 4, 2, DH], BF16, name="cos_rows")
+        sin_rows = head.tile([P, 4, 2, DH], BF16, name="sin_rows")
+        for d in range(2):
+            nc.sync.dma_start(out=cos_rows[:, 0:3, d, :], in_=cos1.rearrange("(a q) c -> q a c", q=P))
+            nc.sync.dma_start(out=sin_rows[:, 0:3, d, :], in_=sin1.rearrange("(a q) c -> q a c", q=P))
+            nc.sync.dma_start(out=cos_rows[:, 3, d, :], in_=cos2)
+            nc.sync.dma_start(out=sin_rows[:, 3, d, :], in_=sin2)
         for w in range(4):
             nc.sync.dma_start(out=bias_rows[4 * w:4 * w + 4, :], in_=biases[w].rearrange("(hp x) -> hp x", x=PAIR))
         for b in range(1, B):
@@ -97,39 +96,40 @@ def tile_dualmultiheadattention_pa_kernel(
         ident_b = const.tile([P, P], BF16, name="ident_b")
         make_identity(nc, ident_b[:])
 
-        table_rows = head.tile([P, 4, 4, DH], BF16, name="table_rows")
-        bias_rows_f = head.tile([P, PAIR], F32, name="bias_rows_f")
         bias_col = const.tile([P, 2, P], F32, name="bias_col")
         tables = const.tile([P, 4, 6 * P + CHUNK], BF16, name="tables")
 
         def constants():
-            for hh in range(2):
-                for (t, rows, parity, sign) in ((0, cos_rows, 0, 1.0), (1, sin_rows, 0, -1.0), (2, cos_rows, 1, 1.0), (3, sin_rows, 1, 1.0)):
-                    nc.vector.tensor_scalar(out=table_rows[:, t, :, hh * 64:(hh + 1) * 64], in0=rows[:, :, parity:DH:2],
-                                            scalar1=sign, scalar2=None, op0=ALU.mult)
-            nc.vector.tensor_copy(out=bias_rows_f[:], in_=bias_rows[:])
-            bias_ps = tps.tile([P, 2, P], F32, name="bias_ps", tag="tp")
+            bias_ps = tps.tile([P, 2, P], BF16, name="bias_ps", tag="tp")
             for e in range(2):
-                nc.tensor.transpose(bias_ps[:, e, :], bias_rows_f[:, e:PAIR:2], ident_f[:])
+                nc.tensor.transpose(bias_ps[:, e, :], bias_rows[:, e:PAIR:2], ident_b[:])
             nc.scalar.copy(out=bias_col[:], in_=bias_ps[:])
 
+        factor_of_product = ((cos_rows, 0, 1.0), (sin_rows, 1, 1.0), (sin_rows, 0, -1.0), (cos_rows, 1, 1.0))
         table_ps = {}
 
         def table_turn(t):
+            rows, parity, sign = factor_of_product[t]
             ps = tps.tile([P, 2 * CHUNK], BF16, name="table_ps", tag="tp")
-            for a in range(3):
-                nc.tensor.transpose(ps[:, a * P:(a + 1) * P], table_rows[:, t, a, :], ident_b[:])
-            for r in range(4):
-                nc.tensor.transpose(ps[:, N1 + r * P:N1 + (r + 1) * P], table_rows[:, t, 3, :], ident_b[:])
+            for place in range(7):
+                a = min(place, 3)
+                nc.tensor.transpose(ps[:, place * P:(place + 1) * P],
+                                    rows[:, a, :, :].rearrange("p d c -> p (d c)")[:, parity:2 * DH:2], ident_b[:])
             table_ps[t] = ps
 
         def table_leave(t, part):
+            sign = factor_of_product[t][2]
             ps = table_ps[t]
             if part < 2:
-                nc.scalar.copy(out=tables[:, t, N1 * part:N1 * (part + 1)].rearrange("m (i p) -> m i p", i=3),
-                               in_=ps[:, 0:N1].rearrange("m (p i) -> m i p", i=3))
+                to = tables[:, t, N1 * part:N1 * (part + 1)].rearrange("m (i p) -> m i p", i=3)
+                turned_rows = ps[:, 0:N1].rearrange("m (p i) -> m i p", i=3)
             else:
-                nc.scalar.copy(out=tables[:, t, 2 * N1:2 * N1 + CHUNK], in_=ps[:, N1:N1 + CHUNK])
+                to = tables[:, t, 2 * N1:2 * N1 + CHUNK]
+                turned_rows = ps[:, N1:N1 + CHUNK]
+            if sign == 1.0:
+                nc.scalar.copy(out=to, in_=turned_rows)
+            else:
+                nc.scalar.activation(out=to, in_=turned_rows, func=ACT.Copy, scale=sign)
 
         x_grouped = {}
         x_codes = {}
@@ -214,29 +214,29 @@ def tile_dualmultiheadattention_pa_kernel(
                                     rhs=xc[:, g, :].bitcast(FP8X4), rhs_scale=xs[:, g, :], start=(g == 0), stop=(g == 1))
             banks[(k, e)] = bank
 
-        def product(k, t):
+        def product(k, e):
             gi, chunk = units[k]
             w, hp = groups[gi]
-            e = BANK_OF_PRODUCT[t]
             at = 6 * P if chunk == X2_CHUNK else P * chunk
-            u = up.tile([P, CHUNK], F32, name="product%d" % t, tag="product%d" % t)
-            nc.vector.scalar_tensor_tensor(out=u[:], in0=banks[(k, e)][:], scalar=bias_col[:, e, 4 * w + hp:4 * w + hp + 1],
-                                           in1=tables[:, t, at:at + CHUNK], op0=ALU.add, op1=ALU.mult)
-            products[(k, t)] = u
+            u = up.tile([P, 2, CHUNK], F32, name="products%d" % e, tag="products%d" % e)
+            nc.vector.scalar_tensor_tensor(out=u[:], in0=banks[(k, e)][:].unsqueeze(1).to_broadcast([P, 2, CHUNK]),
+                                           scalar=bias_col[:, e, 4 * w + hp:4 * w + hp + 1],
+                                           in1=tables[:, 2 * e:2 * e + 2, at:at + CHUNK], op0=ALU.add, op1=ALU.mult)
+            products[(k, e)] = u
 
         def add_odd(k):
-            nc.gpsimd.tensor_tensor(out=products[(k, 2)][:], in0=products[(k, 2)][:], in1=products[(k, 3)][:], op=ALU.add)
+            nc.gpsimd.tensor_tensor(out=products[(k, 1)][:, 1, :], in0=products[(k, 1)][:, 1, :], in1=products[(k, 0)][:, 1, :], op=ALU.add)
 
         def turn(k, half):
             ps = tps.tile([P, 2, 2, P], F32, name="turned", tag="tp")
             for ib in range(2):
                 cols = slice((2 * half + ib) * P, (2 * half + ib + 1) * P)
-                for e in range(2):
-                    if e == 0 or k == last:
-                        nc.tensor.matmul(out=ps[:, e, ib, :], lhsT=products[(k, 2 * e)][:, cols], rhs=ident_f[:], is_transpose=True, start=True, stop=False)
-                        nc.tensor.matmul(out=ps[:, e, ib, :], lhsT=products[(k, 2 * e + 1)][:, cols], rhs=ident_f[:], is_transpose=True, start=False, stop=True)
+                for q in range(2):
+                    if q == 0 or k == last:
+                        nc.tensor.matmul(out=ps[:, q, ib, :], lhsT=products[(k, 0)][:, q, cols], rhs=ident_f[:], is_transpose=True, start=True, stop=False)
+                        nc.tensor.matmul(out=ps[:, q, ib, :], lhsT=products[(k, 1)][:, q, cols], rhs=ident_f[:], is_transpose=True, start=False, stop=True)
                     else:
-                        nc.tensor.transpose(ps[:, e, ib, :], products[(k, 2)][:, cols], ident_f[:])
+                        nc.tensor.transpose(ps[:, q, ib, :], products[(k, 1)][:, q, cols], ident_f[:])
             turned[(k, half)] = ps
 
         def leave(k, half):
@@ -275,7 +275,8 @@ def tile_dualmultiheadattention_pa_kernel(
             if 0 <= n - X2_FIRST_SLOT < B:
                 x_turn(X2_CHUNK, n - X2_FIRST_SLOT, x2_sb[:, n - X2_FIRST_SLOT, :])
             if live:
-                product(n, PRODUCT_ORDER[0])
+                product(n, 1)
+                product(n, 0)
             for gi in range(len(groups)):
                 if n == w_quantise_slot(gi):
                     w_quantise(gi)
@@ -283,16 +284,10 @@ def tile_dualmultiheadattention_pa_kernel(
                 x_quantise(2)
             if n == X2_FIRST_SLOT + B:
                 x_quantise(X2_CHUNK)
-            if live:
-                product(n, PRODUCT_ORDER[1])
-                if n < last:
-                    add_odd(n)
-                product(n, PRODUCT_ORDER[2])
+            if live and n < last:
+                add_odd(n)
             if ahead:
                 passes(n + AHEAD, 0)
-            if live:
-                product(n, PRODUCT_ORDER[3])
-            if ahead:
                 passes(n + AHEAD, 1)
             if behind:
                 leave(n - BEHIND, 0)

@@ -73,19 +73,21 @@ def tile_dualmultiheadattention_pa_kernel(
                 nc.sync.dma_start(out=rows[:], in_=weights[w][K_PASS * g:K_PASS * (g + 1), :].rearrange("(p r) c -> p r c", r=4))
                 w_raw[(w, g)] = rows
 
-        load_x1(0)
         cos_rows = head.tile([P, 4, 2, DH], BF16, name="cos_rows")
         sin_rows = head.tile([P, 4, 2, DH], BF16, name="sin_rows")
         for d in range(2):
+            nc.scalar.dma_start(out=cos_rows[:, 3, d, :], in_=cos2)
+            nc.scalar.dma_start(out=sin_rows[:, 3, d, :], in_=sin2)
+        load_x1(0)
+        for d in range(2):
             nc.sync.dma_start(out=cos_rows[:, 0:3, d, :], in_=cos1.rearrange("(a q) c -> q a c", q=P))
             nc.sync.dma_start(out=sin_rows[:, 0:3, d, :], in_=sin1.rearrange("(a q) c -> q a c", q=P))
-            nc.sync.dma_start(out=cos_rows[:, 3, d, :], in_=cos2)
-            nc.sync.dma_start(out=sin_rows[:, 3, d, :], in_=sin2)
         for w in range(4):
             nc.sync.dma_start(out=bias_rows[4 * w:4 * w + 4, :], in_=biases[w].rearrange("(hp x) -> hp x", x=PAIR))
-        for b in range(1, B):
-            load_x1(b)
+        load_x1(1)
         load_w(W_ORDER[0])
+        load_x1(2)
+        load_x1(3)
         x2_sb = head.tile([P, B, D], BF16, name="x2_sb")
         nc.sync.dma_start(out=x2_sb[:], in_=x_2.rearrange("b p k -> p b k"))
         load_w(W_ORDER[1])
@@ -110,22 +112,28 @@ def tile_dualmultiheadattention_pa_kernel(
 
         def table_turn(t):
             rows, parity, sign = factor_of_product[t]
-            ps = tps.tile([P, 2 * CHUNK], BF16, name="table_ps", tag="tp")
-            for place in range(7):
-                a = min(place, 3)
-                nc.tensor.transpose(ps[:, place * P:(place + 1) * P],
+            ps = tps.tile([P, N1], BF16, name="table_ps", tag="tp")
+            for a in range(3):
+                nc.tensor.transpose(ps[:, a * P:(a + 1) * P],
                                     rows[:, a, :, :].rearrange("p d c -> p (d c)")[:, parity:2 * DH:2], ident_b[:])
             table_ps[t] = ps
 
+        def table2_turn():
+            ps = tps.tile([P, 4, P], BF16, name="table2_ps", tag="tp")
+            for t in range(4):
+                rows, parity = factor_of_product[t][0:2]
+                nc.tensor.transpose(ps[:, t, :], rows[:, 3, :, :].rearrange("p d c -> p (d c)")[:, parity:2 * DH:2], ident_b[:])
+            table_ps[X2_CHUNK + 1] = ps
+
         def table_leave(t, part):
             sign = factor_of_product[t][2]
-            ps = table_ps[t]
+            ps = table_ps[t if part < 2 else X2_CHUNK + 1]
             if part < 2:
                 to = tables[:, t, N1 * part:N1 * (part + 1)].rearrange("m (i p) -> m i p", i=3)
-                turned_rows = ps[:, 0:N1].rearrange("m (p i) -> m i p", i=3)
+                turned_rows = ps[:].rearrange("m (p i) -> m i p", i=3)
             else:
-                to = tables[:, t, 2 * N1:2 * N1 + CHUNK]
-                turned_rows = ps[:, N1:N1 + CHUNK]
+                to = tables[:, t, 2 * N1:2 * N1 + CHUNK].rearrange("m (r p) -> m r p", r=B)
+                turned_rows = ps[:, t, :].unsqueeze(1).to_broadcast([P, B, P])
             if sign == 1.0:
                 nc.scalar.copy(out=to, in_=turned_rows)
             else:
@@ -180,22 +188,7 @@ def tile_dualmultiheadattention_pa_kernel(
             w_codes[gi] = (codes, scales)
 
         def w_quantise_slot(gi):
-            return max(2 * gi - 3, gi) if gi > 0 else -3
-
-        for blk in range(BLOCKS_1):
-            x1_block(blk)
-            if blk == 1:
-                constants()
-            if blk >= 2:
-                table_leave((blk - 2) // 3, (blk - 2) % 3)
-            if blk in (6, 7):
-                w_piece(blk - 6)
-            if blk % 3 == 1:
-                table_turn(blk // 3)
-            if blk in (5, 9):
-                x_quantise((blk - 5) // 4)
-        table_leave(3, 1)
-        table_leave(3, 2)
+            return max(2 * gi - 3, gi)
 
         units = [(gi, chunk) for gi in range(len(groups)) for chunk in ((X2_CHUNK,) if groups[gi][0] >= 2 else (0, 1, 2))]
         last = len(units) - 1
@@ -248,7 +241,7 @@ def tile_dualmultiheadattention_pa_kernel(
                 if chunk == X2_CHUNK:
                     b, i = 0, blk
                     if blk == 0:
-                        o2 = op.tile([P, 2, B, DH], F32, name="out2_sb", tag="out2_sb", bufs=2)
+                        o2 = op.tile([P, 2, B, DH], F32, name="out2_sb", tag="out2_sb", bufs=4)
                         out_sb[b] = o2
                 else:
                     b, i = (4 * chunk + blk) // 3, (4 * chunk + blk) % 3
@@ -265,9 +258,30 @@ def tile_dualmultiheadattention_pa_kernel(
                 for hh in range(2):
                     nc.sync.dma_start(out=outs[w][:, 2 * hp + hh, N1:N1 + N2, :].rearrange("b p c -> p b c"), in_=out_sb[0][:, hh, :, :])
 
+        table2_turn()
+        for t in range(4):
+            table_leave(t, 2)
+        for blk in range(BLOCKS_1):
+            if blk == BLOCKS_1 - 2:
+                passes(0, 0)
+                passes(0, 1)
+            x1_block(blk)
+            if blk == 1:
+                constants()
+            if 2 <= blk < 10:
+                table_leave((blk - 2) // 2, (blk - 2) % 2)
+            if blk in (5, 6):
+                w_piece(blk - 5)
+            if blk in (1, 3, 5, 7):
+                table_turn(blk // 2)
+            if blk in (5, 9):
+                x_quantise((blk - 5) // 4)
+            if blk == BLOCKS_1 - 3:
+                w_quantise(0)
+
         for n in range(-PIECE_LEAD, len(units) + BEHIND):
             live = 0 <= n <= last
-            ahead = 0 <= n + AHEAD <= last
+            ahead = 1 <= n + AHEAD <= last
             behind = 0 <= n - BEHIND <= last
             if behind:
                 turn(n - BEHIND, 0)
@@ -277,10 +291,10 @@ def tile_dualmultiheadattention_pa_kernel(
             if live:
                 product(n, 1)
                 product(n, 0)
-            for gi in range(len(groups)):
+            for gi in range(1, len(groups)):
                 if n == w_quantise_slot(gi):
                     w_quantise(gi)
-            if n == w_quantise_slot(0):
+            if n == 0:
                 x_quantise(2)
             if n == X2_FIRST_SLOT + B:
                 x_quantise(X2_CHUNK)

@@ -97,6 +97,8 @@ def tile_dualmultiheadattention_pa_kernel(
         make_identity(nc, ident_f[:])
         ident_b = const.tile([P, P], BF16, name="ident_b")
         make_identity(nc, ident_b[:])
+        zeros = const.tile([P, CHUNK], BF16, name="zeros")
+        nc.gpsimd.memset(zeros[:], 0.0)
 
         bias_col = const.tile([P, 2, P], F32, name="bias_col")
         tables = const.tile([P, 4, 6 * P + CHUNK], BF16, name="tables")
@@ -258,6 +260,11 @@ def tile_dualmultiheadattention_pa_kernel(
                 for hh in range(2):
                     nc.sync.dma_start(out=outs[w][:, 2 * hp + hh, N1:N1 + N2, :].rearrange("b p c -> p b c"), in_=out_sb[0][:, hh, :, :])
 
+        def keep_clock_up(blk):
+            idle = accp.tile([P, CHUNK], F32, name="idle", tag="bank%d" % (blk % 2))
+            for again in range(2):
+                nc.tensor.matmul(out=idle[:], lhsT=ident_b[:], rhs=zeros[:], start=True, stop=True)
+
         table2_turn()
         for t in range(4):
             table_leave(t, 2)
@@ -265,6 +272,8 @@ def tile_dualmultiheadattention_pa_kernel(
             if blk == BLOCKS_1 - 2:
                 passes(0, 0)
                 passes(0, 1)
+            if blk < BLOCKS_1 - 2:
+                keep_clock_up(blk)
             x1_block(blk)
             if blk == 1:
                 constants()

@@ -67,11 +67,13 @@ def tile_dualmultiheadattention_pa_kernel(
 
         w_raw = {}
 
-        def load_w(w):
+        def load_w(w, first=0, width=E):
             for g in range(2):
-                rows = wrawp.tile([P, 4, E], BF16, name="w_raw", tag="w_raw")
-                nc.sync.dma_start(out=rows[:], in_=weights[w][K_PASS * g:K_PASS * (g + 1), :].rearrange("(p r) c -> p r c", r=4))
-                w_raw[(w, g)] = rows
+                if first == 0:
+                    rows = wrawp.tile([P, 4, E], BF16, name="w_raw", tag="w_raw")
+                    w_raw[(w, g)] = rows
+                nc.sync.dma_start(out=w_raw[(w, g)][:, :, first:first + width],
+                                  in_=weights[w][K_PASS * g:K_PASS * (g + 1), first:first + width].rearrange("(p r) c -> p r c", r=4))
 
         cos_rows = head.tile([P, 4, 2, DH], BF16, name="cos_rows")
         sin_rows = head.tile([P, 4, 2, DH], BF16, name="sin_rows")
@@ -82,12 +84,13 @@ def tile_dualmultiheadattention_pa_kernel(
         for d in range(2):
             nc.sync.dma_start(out=cos_rows[:, 0:3, d, :], in_=cos1.rearrange("(a q) c -> q a c", q=P))
             nc.sync.dma_start(out=sin_rows[:, 0:3, d, :], in_=sin1.rearrange("(a q) c -> q a c", q=P))
-        for w in range(4):
-            nc.sync.dma_start(out=bias_rows[4 * w:4 * w + 4, :], in_=biases[w].rearrange("(hp x) -> hp x", x=PAIR))
         load_x1(1)
-        load_w(W_ORDER[0])
+        load_w(W_ORDER[0], 0, PAIR)
         load_x1(2)
         load_x1(3)
+        for w in range(4):
+            nc.sync.dma_start(out=bias_rows[4 * w:4 * w + 4, :], in_=biases[w].rearrange("(hp x) -> hp x", x=PAIR))
+        load_w(W_ORDER[0], PAIR, E - PAIR)
         x2_sb = head.tile([P, B, D], BF16, name="x2_sb")
         nc.sync.dma_start(out=x2_sb[:], in_=x_2.rearrange("b p k -> p b k"))
         load_w(W_ORDER[1])
@@ -219,15 +222,19 @@ def tile_dualmultiheadattention_pa_kernel(
                                            in1=tables[:, 2 * e:2 * e + 2, at:at + CHUNK], op0=ALU.add, op1=ALU.mult)
             products[(k, e)] = u
 
-        def add_odd(k):
-            nc.gpsimd.tensor_tensor(out=products[(k, 1)][:, 1, :], in0=products[(k, 1)][:, 1, :], in1=products[(k, 0)][:, 1, :], op=ALU.add)
+        def gpsimd_adds_both(k):
+            return k % 2 == 1 and 3 <= k < last
+
+        def add_sums(k):
+            q0 = 0 if gpsimd_adds_both(k) else 1
+            nc.gpsimd.tensor_tensor(out=products[(k, 1)][:, q0:2, :], in0=products[(k, 1)][:, q0:2, :], in1=products[(k, 0)][:, q0:2, :], op=ALU.add)
 
         def turn(k, half):
             ps = tps.tile([P, 2, 2, P], F32, name="turned", tag="tp")
             for ib in range(2):
                 cols = slice((2 * half + ib) * P, (2 * half + ib + 1) * P)
                 for q in range(2):
-                    if q == 0 or k == last:
+                    if (q == 0 and not gpsimd_adds_both(k)) or k == last:
                         nc.tensor.matmul(out=ps[:, q, ib, :], lhsT=products[(k, 0)][:, q, cols], rhs=ident_f[:], is_transpose=True, start=True, stop=False)
                         nc.tensor.matmul(out=ps[:, q, ib, :], lhsT=products[(k, 1)][:, q, cols], rhs=ident_f[:], is_transpose=True, start=False, stop=True)
                     else:
@@ -275,7 +282,7 @@ def tile_dualmultiheadattention_pa_kernel(
             if blk < BLOCKS_1 - 2:
                 keep_clock_up(blk)
             x1_block(blk)
-            if blk == 1:
+            if blk == 8:
                 constants()
             if 2 <= blk < 10:
                 table_leave((blk - 2) // 2, (blk - 2) % 2)
@@ -308,7 +315,7 @@ def tile_dualmultiheadattention_pa_kernel(
             if n == X2_FIRST_SLOT + B:
                 x_quantise(X2_CHUNK)
             if live and n < last:
-                add_odd(n)
+                add_sums(n)
             if ahead:
                 passes(n + AHEAD, 0)
                 passes(n + AHEAD, 1)

@@ -54,10 +54,12 @@ def tile_dualmultiheadattention_pa_kernel(
         tps = ctx.enter_context(tc.psum_pool(name="tps", bufs=4))
         ctx.enter_context(tc.manual_schedule())
 
+        ident_f = const.tile([P, P], F32, name="ident_f")
+        make_identity(nc, ident_f[:])
         bias_rows = head.tile([P, PAIR], BF16, name="bias_rows")
         nc.gpsimd.memset(bias_rows[:], 0.0)
-        scale_all = head.tile([P, D], F32, name="scale_all")
-        nc.sync.dma_start(out=scale_all[:], in_=x_1_scale.rearrange("a b k -> (a b k)").partition_broadcast(P))
+        scale_cols = head.tile([P, 8], F32, name="scale_cols")
+        nc.sync.dma_start(out=scale_cols[:], in_=x_1_scale.rearrange("a b (p j) -> (a b p) j", j=8))
         x1_bytes_sb = {}
 
         def load_x1(b):
@@ -96,8 +98,6 @@ def tile_dualmultiheadattention_pa_kernel(
         load_w(W_ORDER[1])
         load_w(W_ORDER[2])
 
-        ident_f = const.tile([P, P], F32, name="ident_f")
-        make_identity(nc, ident_f[:])
         ident_b = const.tile([P, P], BF16, name="ident_b")
         make_identity(nc, ident_b[:])
         zeros = const.tile([P, CHUNK], BF16, name="zeros")
@@ -143,6 +143,19 @@ def tile_dualmultiheadattention_pa_kernel(
                 nc.scalar.copy(out=to, in_=turned_rows)
             else:
                 nc.scalar.activation(out=to, in_=turned_rows, func=ACT.Copy, scale=sign)
+
+        scale_all = head.tile([P, D], F32, name="scale_all")
+
+        def spread_scales():
+            for h in range(2):
+                ps = tps.tile([P, 4, P], F32, name="scale_ps", tag="tp")
+                for j in range(4):
+                    nc.tensor.transpose(ps[:, j, :], scale_cols[:, 4 * h + j:4 * h + j + 1].to_broadcast([P, P]), ident_f[:])
+                to = scale_all[:].rearrange("m (p j) -> m p j", j=8)[:, :, 4 * h:4 * h + 4]
+                if h == 0:
+                    nc.scalar.copy(out=to, in_=ps[:].rearrange("m j p -> m p j"))
+                else:
+                    nc.vector.tensor_copy(out=to, in_=ps[:].rearrange("m j p -> m p j"))
 
         x_grouped = {}
         x_codes = {}
@@ -272,6 +285,7 @@ def tile_dualmultiheadattention_pa_kernel(
             for again in range(2):
                 nc.tensor.matmul(out=idle[:], lhsT=ident_b[:], rhs=zeros[:], start=True, stop=True)
 
+        spread_scales()
         table2_turn()
         for t in range(4):
             table_leave(t, 2)

@@ -62,10 +62,12 @@ def tile_dualmultiheadattention_pa_kernel(
         nc.sync.dma_start(out=scale_cols[:], in_=x_1_scale.rearrange("a b (p j) -> (a b p) j", j=8))
         x1_bytes_sb = {}
 
-        def load_x1(b):
-            held = head.tile([P, 3 * D], U8, name="x1_bytes_sb%d" % b, tag="x1_bytes_sb%d" % b)
-            nc.sync.dma_start(out=held[:], in_=x_1_bytes[b].rearrange("(p i) k -> p (i k)", i=3))
-            x1_bytes_sb[b] = held
+        def load_x1(b, first=0, width=3 * D):
+            if first == 0:
+                held = head.tile([P, 3 * D], U8, name="x1_bytes_sb%d" % b, tag="x1_bytes_sb%d" % b)
+                x1_bytes_sb[b] = held
+            nc.sync.dma_start(out=x1_bytes_sb[b][:, first:first + width],
+                              in_=x_1_bytes[b].rearrange("(p i) k -> p (i k)", i=3)[:, first:first + width])
 
         w_raw = {}
 
@@ -79,14 +81,14 @@ def tile_dualmultiheadattention_pa_kernel(
 
         cos_rows = head.tile([P, 4, 2, DH], BF16, name="cos_rows")
         sin_rows = head.tile([P, 4, 2, DH], BF16, name="sin_rows")
-        for d in range(2):
-            nc.scalar.dma_start(out=cos_rows[:, 3, d, :], in_=cos2)
-            nc.scalar.dma_start(out=sin_rows[:, 3, d, :], in_=sin2)
-        load_x1(0)
+        nc.scalar.dma_start(out=cos_rows[:, 3, :, :], in_=cos2.unsqueeze(1).to_broadcast([P, 2, DH]))
+        nc.scalar.dma_start(out=sin_rows[:, 3, :, :], in_=sin2.unsqueeze(1).to_broadcast([P, 2, DH]))
+        load_x1(0, 0, D)
+        load_x1(0, D, 2 * D)
+        load_x1(1)
         for d in range(2):
             nc.sync.dma_start(out=cos_rows[:, 0:3, d, :], in_=cos1.rearrange("(a q) c -> q a c", q=P))
             nc.sync.dma_start(out=sin_rows[:, 0:3, d, :], in_=sin1.rearrange("(a q) c -> q a c", q=P))
-        load_x1(1)
         load_w(W_ORDER[0], 0, PAIR)
         load_x1(2)
         load_x1(3)

@@ -27,7 +27,8 @@ W_ORDER = (0, 2, 1, 3)
 AHEAD = 2
 BEHIND = 2
 PIECE_LEAD = 6
-X2_FIRST_SLOT = 3
+TURN_FREE_SLOTS = (0, 1)
+X2_QUANTISE_SLOT = 4
 
 
 def tile_dualmultiheadattention_pa_kernel(
@@ -58,8 +59,8 @@ def tile_dualmultiheadattention_pa_kernel(
         make_identity(nc, ident_f[:])
         bias_rows = head.tile([P, PAIR], BF16, name="bias_rows")
         nc.gpsimd.memset(bias_rows[:], 0.0)
-        scale_cols = head.tile([P, 8], F32, name="scale_cols")
-        nc.sync.dma_start(out=scale_cols[:], in_=x_1_scale.rearrange("a b (p j) -> (a b p) j", j=8))
+        scale_cols = head.tile([P, 2, 4], F32, name="scale_cols")
+        nc.sync.dma_start(out=scale_cols[:], in_=x_1_scale.rearrange("a b (g p j) -> (a b p) g j", g=2, j=4))
         x1_bytes_sb = {}
 
         def load_x1(b, first=0, width=3 * D):
@@ -149,15 +150,11 @@ def tile_dualmultiheadattention_pa_kernel(
         scale_all = head.tile([P, D], F32, name="scale_all")
 
         def spread_scales():
-            for h in range(2):
+            for g in range(2):
                 ps = tps.tile([P, 4, P], F32, name="scale_ps", tag="tp")
                 for j in range(4):
-                    nc.tensor.transpose(ps[:, j, :], scale_cols[:, 4 * h + j:4 * h + j + 1].to_broadcast([P, P]), ident_f[:])
-                to = scale_all[:].rearrange("m (p j) -> m p j", j=8)[:, :, 4 * h:4 * h + 4]
-                if h == 0:
-                    nc.scalar.copy(out=to, in_=ps[:].rearrange("m j p -> m p j"))
-                else:
-                    nc.vector.tensor_copy(out=to, in_=ps[:].rearrange("m j p -> m p j"))
+                    nc.tensor.transpose(ps[:, j, :], scale_cols[:, g, j:j + 1].to_broadcast([P, P]), ident_f[:])
+                nc.scalar.copy(out=scale_all[:, K_PASS * g:K_PASS * (g + 1)].rearrange("m (p j) -> m p j", j=4), in_=ps[:].rearrange("m j p -> m p j"))
 
         x_grouped = {}
         x_codes = {}
@@ -184,21 +181,27 @@ def tile_dualmultiheadattention_pa_kernel(
         def x1_block(blk):
             b, i = blk // 3, blk % 3
             x_bf16 = xbp.tile([P, D], BF16, name="x_bf16", tag="x_bf16", align_bytes=64)
-            nc.vector.tensor_tensor(out=x_bf16[:], in0=x1_bytes_sb[b][:, i * D:(i + 1) * D].bitcast(FP8), in1=scale_all[:], op=ALU.mult)
+            for first, width in ((0, K_PASS), (K_PASS, K_PASS)) if blk == 0 else ((0, D),):
+                nc.vector.tensor_tensor(out=x_bf16[:, first:first + width], in0=x1_bytes_sb[b][:, i * D + first:i * D + first + width].bitcast(FP8),
+                                        in1=scale_all[:, first:first + width], op=ALU.mult)
             x_turn(blk // 4, blk % 4, x_bf16[:])
 
         groups = [(w, hp) for w in W_ORDER for hp in range(H // 2)]
         w_grouped = {}
         w_codes = {}
 
-        def w_piece(j):
+        def w_piece(j, on_gpsimd=False):
             gi, g = j // 2, j % 2
             w, hp = groups[gi]
             if g == 0:
                 grouped = wgp.tile([P, 2, 4 * PAIR], BF16, name="w_grouped", tag="w_grouped", align_bytes=64)
                 w_grouped[gi] = grouped
-            nc.scalar.copy(out=w_grouped[gi][:, g, :].rearrange("p (e m r) -> p e m r", e=2, r=4),
-                           in_=w_raw[(w, g)][:, :, hp * PAIR:(hp + 1) * PAIR].rearrange("p r (m e) -> p e m r", e=2))
+            to = w_grouped[gi][:, g, :].rearrange("p (e m r) -> p e m r", e=2, r=4)
+            rows = w_raw[(w, g)][:, :, hp * PAIR:(hp + 1) * PAIR].rearrange("p r (m e) -> p e m r", e=2)
+            if on_gpsimd:
+                nc.gpsimd.tensor_scalar(out=to, in0=rows, scalar1=1.0, scalar2=0.0, op0=ALU.mult, op1=ALU.add)
+            else:
+                nc.scalar.copy(out=to, in_=rows)
 
         def w_quantise(gi):
             codes = wcp.tile([P, 2, PAIR], U32, name="w_codes", tag="w_codes", align_bytes=64)
@@ -227,14 +230,17 @@ def tile_dualmultiheadattention_pa_kernel(
                                     rhs=xc[:, g, :].bitcast(FP8X4), rhs_scale=xs[:, g, :], start=(g == 0), stop=(g == 1))
             banks[(k, e)] = bank
 
-        def product(k, e):
+        def product(k, e, first=0, width=CHUNK):
             gi, chunk = units[k]
             w, hp = groups[gi]
             at = 6 * P if chunk == X2_CHUNK else P * chunk
-            u = up.tile([P, 2, CHUNK], F32, name="products%d" % e, tag="products%d" % e)
-            nc.vector.scalar_tensor_tensor(out=u[:], in0=banks[(k, e)][:].unsqueeze(1).to_broadcast([P, 2, CHUNK]),
+            u = up.tile([P, 2, width], F32, name="products%d" % e, tag="products%d" % e)
+            nc.vector.scalar_tensor_tensor(out=u[:], in0=banks[(k, e)][:, first:first + width].unsqueeze(1).to_broadcast([P, 2, width]),
                                            scalar=bias_col[:, e, 4 * w + hp:4 * w + hp + 1],
-                                           in1=tables[:, 2 * e:2 * e + 2, at:at + CHUNK], op0=ALU.add, op1=ALU.mult)
+                                           in1=tables[:, 2 * e:2 * e + 2, at + first:at + first + width], op0=ALU.add, op1=ALU.mult)
+            for half in range(2):
+                if first <= half * 2 * P < first + width:
+                    products[(k, e, half)] = u[:, :, half * 2 * P - first:(half + 1) * 2 * P - first]
             products[(k, e)] = u
 
         def gpsimd_adds_both(k):
@@ -247,13 +253,13 @@ def tile_dualmultiheadattention_pa_kernel(
         def turn(k, half):
             ps = tps.tile([P, 2, 2, P], F32, name="turned", tag="tp")
             for ib in range(2):
-                cols = slice((2 * half + ib) * P, (2 * half + ib + 1) * P)
+                cols = slice(ib * P, (ib + 1) * P)
                 for q in range(2):
-                    if (q == 0 and not gpsimd_adds_both(k)) or k == last:
-                        nc.tensor.matmul(out=ps[:, q, ib, :], lhsT=products[(k, 0)][:, q, cols], rhs=ident_f[:], is_transpose=True, start=True, stop=False)
-                        nc.tensor.matmul(out=ps[:, q, ib, :], lhsT=products[(k, 1)][:, q, cols], rhs=ident_f[:], is_transpose=True, start=False, stop=True)
+                    if (q == 0 and not gpsimd_adds_both(k)) or k >= last - 1:
+                        nc.tensor.matmul(out=ps[:, q, ib, :], lhsT=products[(k, 0, half)][:, q, cols], rhs=ident_f[:], is_transpose=True, start=True, stop=False)
+                        nc.tensor.matmul(out=ps[:, q, ib, :], lhsT=products[(k, 1, half)][:, q, cols], rhs=ident_f[:], is_transpose=True, start=False, stop=True)
                     else:
-                        nc.tensor.transpose(ps[:, q, ib, :], products[(k, 1)][:, q, cols], ident_f[:])
+                        nc.tensor.transpose(ps[:, q, ib, :], products[(k, 1, half)][:, q, cols], ident_f[:])
             turned[(k, half)] = ps
 
         def leave(k, half):
@@ -278,7 +284,9 @@ def tile_dualmultiheadattention_pa_kernel(
                 if chunk != X2_CHUNK and i == 2:
                     nc.sync.dma_start(out=outs[w][b, 2 * hp:2 * hp + 2, 0:N1, :].rearrange("hh (p i) c -> p hh (i c)", i=3),
                                       in_=out_sb[b][:].rearrange("p hh i c -> p hh (i c)"))
-            if chunk == X2_CHUNK and half == 1:
+                if k == last:
+                    nc.sync.dma_start(out=outs[w][i, 2 * hp:2 * hp + 2, N1:N1 + N2, :].rearrange("hh p c -> p hh c"), in_=out_sb[0][:, :, i, :])
+            if chunk == X2_CHUNK and half == 1 and k < last:
                 for hh in range(2):
                     nc.sync.dma_start(out=outs[w][:, 2 * hp + hh, N1:N1 + N2, :].rearrange("b p c -> p b c"), in_=out_sb[0][:, hh, :, :])
 
@@ -318,19 +326,24 @@ def tile_dualmultiheadattention_pa_kernel(
             if behind:
                 turn(n - BEHIND, 0)
                 turn(n - BEHIND, 1)
-            if 0 <= n - X2_FIRST_SLOT < B:
-                x_turn(X2_CHUNK, n - X2_FIRST_SLOT, x2_sb[:, n - X2_FIRST_SLOT, :])
-            if live:
+            if n in TURN_FREE_SLOTS:
+                for b in (2 * n, 2 * n + 1):
+                    x_turn(X2_CHUNK, b, x2_sb[:, b, :])
+            if live and n < last:
                 product(n, 1)
                 product(n, 0)
+            if n == last:
+                for half in range(2):
+                    product(n, 1, half * 2 * P, 2 * P)
+                    product(n, 0, half * 2 * P, 2 * P)
             for gi in range(1, len(groups)):
                 if n == w_quantise_slot(gi):
                     w_quantise(gi)
             if n == 0:
                 x_quantise(2)
-            if n == X2_FIRST_SLOT + B:
+            if n == X2_QUANTISE_SLOT:
                 x_quantise(X2_CHUNK)
-            if live and n < last:
+            if live and n < last - 1:
                 add_sums(n)
             if ahead:
                 passes(n + AHEAD, 0)
@@ -338,8 +351,8 @@ def tile_dualmultiheadattention_pa_kernel(
             if behind:
                 leave(n - BEHIND, 0)
             if 2 <= n + PIECE_LEAD < 2 * len(groups):
-                w_piece(n + PIECE_LEAD)
-            if n == X2_FIRST_SLOT:
+                w_piece(n + PIECE_LEAD, on_gpsimd=n in TURN_FREE_SLOTS)
+            if n == 3:
                 load_w(W_ORDER[3])
             if behind:
                 leave(n - BEHIND, 1)

@@ -186,7 +186,7 @@ def tile_dualmultiheadattention_pa_kernel(
                                         in1=scale_all[:, first:first + width], op=ALU.mult)
             x_turn(blk // 4, blk % 4, x_bf16[:])
 
-        groups = [(w, hp) for w in W_ORDER for hp in range(H // 2)]
+        groups = [(w, hp) for w in W_ORDER[:2] for hp in range(H // 2)] + [(w, hp) for hp in range(H // 2) for w in W_ORDER[2:]]
         w_grouped = {}
         w_codes = {}
 
@@ -244,7 +244,7 @@ def tile_dualmultiheadattention_pa_kernel(
             products[(k, e)] = u
 
         def gpsimd_adds_both(k):
-            return k % 2 == 1 and 3 <= k < last
+            return k % 2 == 1 and 5 <= k < last - 2
 
         def add_sums(k):
             q0 = 0 if gpsimd_adds_both(k) else 1
@@ -262,33 +262,40 @@ def tile_dualmultiheadattention_pa_kernel(
                         nc.tensor.transpose(ps[:, q, ib, :], products[(k, 1, half)][:, q, cols], ident_f[:])
             turned[(k, half)] = ps
 
+        def empty(to, bank, factor):
+            if factor == 1.0:
+                nc.scalar.copy(out=to, in_=bank)
+            else:
+                nc.scalar.activation(out=to, in_=bank, func=ACT.Copy, scale=factor)
+
         def leave(k, half):
             gi, chunk = units[k]
             w, hp = groups[gi]
             factor = Q_FACTOR if w % 2 == 0 else 1.0
+            if chunk == X2_CHUNK:
+                if half == 0:
+                    o2 = op.tile([P, B, 2, DH], F32, name="out2_sb", tag="out2_sb", bufs=4)
+                    out_sb[0] = o2
+                empty(out_sb[0][:, 2 * half:2 * half + 2, :, :].rearrange("p b hh (j e) -> p (b hh j) e", e=2),
+                      turned[(k, half)][:].rearrange("p e b x -> p (b x) e"), factor)
+                if k == last:
+                    for b in (2 * half, 2 * half + 1):
+                        nc.sync.dma_start(out=outs[w][b, 2 * hp:2 * hp + 2, N1:N1 + N2, :].rearrange("hh p c -> p hh c"), in_=out_sb[0][:, b, :, :])
+                elif half == 1:
+                    for hh in range(2):
+                        nc.sync.dma_start(out=outs[w][:, 2 * hp + hh, N1:N1 + N2, :].rearrange("b p c -> p b c"), in_=out_sb[0][:, :, hh, :])
+                return
             for ib in range(2):
                 blk = 2 * half + ib
-                if chunk == X2_CHUNK:
-                    b, i = 0, blk
-                    if blk == 0:
-                        o2 = op.tile([P, 2, B, DH], F32, name="out2_sb", tag="out2_sb", bufs=4)
-                        out_sb[b] = o2
-                else:
-                    b, i = (4 * chunk + blk) // 3, (4 * chunk + blk) % 3
-                    if i == 0:
-                        o1 = op.tile([P, 2, 3, DH], F32, name="out1_sb", tag="out1_sb", bufs=6)
-                        out_sb[b] = o1
-                nc.scalar.activation(out=out_sb[b][:, :, i, :].rearrange("p hh (j e) -> p hh j e", e=2),
-                                     in_=turned[(k, half)][:, :, ib, :].rearrange("p e (hh j) -> p hh j e", hh=2),
-                                     func=ACT.Copy, scale=factor)
-                if chunk != X2_CHUNK and i == 2:
+                b, i = (4 * chunk + blk) // 3, (4 * chunk + blk) % 3
+                if i == 0:
+                    o1 = op.tile([P, 2, 3, DH], F32, name="out1_sb", tag="out1_sb", bufs=6)
+                    out_sb[b] = o1
+                empty(out_sb[b][:, :, i, :].rearrange("p hh (j e) -> p hh j e", e=2),
+                      turned[(k, half)][:, :, ib, :].rearrange("p e (hh j) -> p hh j e", hh=2), factor)
+                if i == 2:
                     nc.sync.dma_start(out=outs[w][b, 2 * hp:2 * hp + 2, 0:N1, :].rearrange("hh (p i) c -> p hh (i c)", i=3),
                                       in_=out_sb[b][:].rearrange("p hh i c -> p hh (i c)"))
-                if k == last:
-                    nc.sync.dma_start(out=outs[w][i, 2 * hp:2 * hp + 2, N1:N1 + N2, :].rearrange("hh p c -> p hh c"), in_=out_sb[0][:, :, i, :])
-            if chunk == X2_CHUNK and half == 1 and k < last:
-                for hh in range(2):
-                    nc.sync.dma_start(out=outs[w][:, 2 * hp + hh, N1:N1 + N2, :].rearrange("b p c -> p b c"), in_=out_sb[0][:, hh, :, :])
 
         def keep_clock_up(blk):
             idle = accp.tile([P, CHUNK], F32, name="idle", tag="bank%d" % (blk % 2))
@@ -310,12 +317,12 @@ def tile_dualmultiheadattention_pa_kernel(
                 constants()
             if 2 <= blk < 10:
                 table_leave((blk - 2) // 2, (blk - 2) % 2)
-            if blk in (5, 6):
-                w_piece(blk - 5)
+            if blk in (3, 5):
+                w_piece((blk - 3) // 2)
             if blk in (1, 3, 5, 7):
                 table_turn(blk // 2)
-            if blk in (5, 9):
-                x_quantise((blk - 5) // 4)
+            if blk in (5, 10):
+                x_quantise((blk - 5) // 5)
             if blk == BLOCKS_1 - 3:
                 w_quantise(0)
 
@@ -351,7 +358,7 @@ def tile_dualmultiheadattention_pa_kernel(
             if behind:
                 leave(n - BEHIND, 0)
             if 2 <= n + PIECE_LEAD < 2 * len(groups):
-                w_piece(n + PIECE_LEAD, on_gpsimd=n in TURN_FREE_SLOTS)
+                w_piece(n + PIECE_LEAD, on_gpsimd=n == 0)
             if n == 3:
                 load_w(W_ORDER[3])
             if behind:

from contextlib import ExitStack

import concourse.mybir as mybir
from concourse.masks import make_identity

F32 = mybir.dt.float32
BF16 = mybir.dt.bfloat16
U32 = mybir.dt.uint32
U8 = mybir.dt.uint8
FP8 = mybir.dt.float8_e4m3fn
FP8X4 = mybir.dt.float8_e4m3fn_x4
ALU = mybir.AluOpType
ACT = mybir.ActivationFunctionType

B, N1, N2, D, H, DH = 4, 384, 128, 1024, 8, 128
E = H * DH
P = 128
K_PASS = 512
CHUNK = 512
PAIR = 2 * DH
FLOPS = 2 * B * (N1 + N2) * D * 2 * E
Q_FACTOR = DH ** -0.5

BLOCKS_1 = B * N1 // P
X2_CHUNK = 3
W_ORDER = (0, 2, 1, 3)
AHEAD = 2
BEHIND = 2
PIECE_LEAD = 6
TURN_FREE_SLOTS = (0, 1)
X2_QUANTISE_SLOT = 4


def tile_dualmultiheadattention_pa_kernel(
    tc, x_1_bytes, x_1_scale, x_2, cos1, sin1, cos2, sin2,
    wq1, bq1, wk1, bk1, wq2, bq2, wk2, bk2, out_0, out_1,
):
    nc = tc.nc
    weights = (wq1, wk1, wq2, wk2)
    biases = (bq1, bk1, bq2, bk2)
    outs = (out_0, out_1, out_0, out_1)

    with ExitStack() as ctx:
        const = ctx.enter_context(tc.tile_pool(name="const", bufs=1))
        head = ctx.enter_context(tc.tile_pool(name="head", bufs=1))
        wrawp = ctx.enter_context(tc.tile_pool(name="wrawp", bufs=6))
        wgp = ctx.enter_context(tc.tile_pool(name="wgp", bufs=3))
        wcp = ctx.enter_context(tc.tile_pool(name="wcp", bufs=6))
        xbp = ctx.enter_context(tc.tile_pool(name="xbp", bufs=4))
        xgp = ctx.enter_context(tc.tile_pool(name="xgp", bufs=2))
        xcp = ctx.enter_context(tc.tile_pool(name="xcp", bufs=1))
        up = ctx.enter_context(tc.tile_pool(name="up", bufs=4))
        op = ctx.enter_context(tc.tile_pool(name="op", bufs=2))
        accp = ctx.enter_context(tc.psum_pool(name="accp", bufs=2))
        tps = ctx.enter_context(tc.psum_pool(name="tps", bufs=4))
        ctx.enter_context(tc.manual_schedule())

        ident_f = const.tile([P, P], F32, name="ident_f")
        make_identity(nc, ident_f[:])
        bias_rows = head.tile([P, PAIR], BF16, name="bias_rows")
        nc.gpsimd.memset(bias_rows[:], 0.0)
        scale_cols = head.tile([P, 2, 4], F32, name="scale_cols")
        nc.sync.dma_start(out=scale_cols[:], in_=x_1_scale.rearrange("a b (g p j) -> (a b p) g j", g=2, j=4))
        x1_bytes_sb = {}

        def load_x1(b, first=0, width=3 * D):
            if first == 0:
                held = head.tile([P, 3 * D], U8, name="x1_bytes_sb%d" % b, tag="x1_bytes_sb%d" % b)
                x1_bytes_sb[b] = held
            nc.sync.dma_start(out=x1_bytes_sb[b][:, first:first + width],
                              in_=x_1_bytes[b].rearrange("(p i) k -> p (i k)", i=3)[:, first:first + width])

        w_raw = {}

        def load_w(w, first=0, width=E):
            for g in range(2):
                if first == 0:
                    rows = wrawp.tile([P, 4, E], BF16, name="w_raw", tag="w_raw")
                    w_raw[(w, g)] = rows
                nc.sync.dma_start(out=w_raw[(w, g)][:, :, first:first + width],
                                  in_=weights[w][K_PASS * g:K_PASS * (g + 1), first:first + width].rearrange("(p r) c -> p r c", r=4))

        cos_rows = head.tile([P, 4, 2, DH], BF16, name="cos_rows")
        sin_rows = head.tile([P, 4, 2, DH], BF16, name="sin_rows")
        nc.scalar.dma_start(out=cos_rows[:, 3, :, :], in_=cos2.unsqueeze(1).to_broadcast([P, 2, DH]))
        nc.scalar.dma_start(out=sin_rows[:, 3, :, :], in_=sin2.unsqueeze(1).to_broadcast([P, 2, DH]))
        load_x1(0, 0, D)
        load_x1(0, D, 2 * D)
        load_x1(1)
        for d in range(2):
            nc.sync.dma_start(out=cos_rows[:, 0:3, d, :], in_=cos1.rearrange("(a q) c -> q a c", q=P))
            nc.sync.dma_start(out=sin_rows[:, 0:3, d, :], in_=sin1.rearrange("(a q) c -> q a c", q=P))
        load_w(W_ORDER[0], 0, PAIR)
        load_x1(2)
        load_x1(3)
        for w in range(4):
            nc.sync.dma_start(out=bias_rows[4 * w:4 * w + 4, :], in_=biases[w].rearrange("(hp x) -> hp x", x=PAIR))
        load_w(W_ORDER[0], PAIR, E - PAIR)
        x2_sb = head.tile([P, B, D], BF16, name="x2_sb")
        nc.sync.dma_start(out=x2_sb[:], in_=x_2.rearrange("b p k -> p b k"))
        load_w(W_ORDER[1])
        load_w(W_ORDER[2])

        ident_b = const.tile([P, P], BF16, name="ident_b")
        make_identity(nc, ident_b[:])
        zeros = const.tile([P, CHUNK], BF16, name="zeros")
        nc.gpsimd.memset(zeros[:], 0.0)

        bias_col = const.tile([P, 2, P], F32, name="bias_col")
        tables = const.tile([P, 4, 6 * P + CHUNK], BF16, name="tables")

        def constants():
            bias_ps = tps.tile([P, 2, P], BF16, name="bias_ps", tag="tp")
            for e in range(2):
                nc.tensor.transpose(bias_ps[:, e, :], bias_rows[:, e:PAIR:2], ident_b[:])
            nc.scalar.copy(out=bias_col[:], in_=bias_ps[:])

        factor_of_product = ((cos_rows, 0, 1.0), (sin_rows, 1, 1.0), (sin_rows, 0, -1.0), (cos_rows, 1, 1.0))
        table_ps = {}

        def table_turn(t):
            rows, parity, sign = factor_of_product[t]
            ps = tps.tile([P, N1], BF16, name="table_ps", tag="tp")
            for a in range(3):
                nc.tensor.transpose(ps[:, a * P:(a + 1) * P],
                                    rows[:, a, :, :].rearrange("p d c -> p (d c)")[:, parity:2 * DH:2], ident_b[:])
            table_ps[t] = ps

        def table2_turn():
            ps = tps.tile([P, 4, P], BF16, name="table2_ps", tag="tp")
            for t in range(4):
                rows, parity = factor_of_product[t][0:2]
                nc.tensor.transpose(ps[:, t, :], rows[:, 3, :, :].rearrange("p d c -> p (d c)")[:, parity:2 * DH:2], ident_b[:])
            table_ps[X2_CHUNK + 1] = ps

        def table_leave(t, part):
            sign = factor_of_product[t][2]
            ps = table_ps[t if part < 2 else X2_CHUNK + 1]
            if part < 2:
                to = tables[:, t, N1 * part:N1 * (part + 1)].rearrange("m (i p) -> m i p", i=3)
                turned_rows = ps[:].rearrange("m (p i) -> m i p", i=3)
            else:
                to = tables[:, t, 2 * N1:2 * N1 + CHUNK].rearrange("m (r p) -> m r p", r=B)
                turned_rows = ps[:, t, :].unsqueeze(1).to_broadcast([P, B, P])
            if sign == 1.0:
                nc.scalar.copy(out=to, in_=turned_rows)
            else:
                nc.scalar.activation(out=to, in_=turned_rows, func=ACT.Copy, scale=sign)

        scale_all = head.tile([P, D], F32, name="scale_all")

        def spread_scales():
            for g in range(2):
                ps = tps.tile([P, 4, P], F32, name="scale_ps", tag="tp")
                for j in range(4):
                    nc.tensor.transpose(ps[:, j, :], scale_cols[:, g, j:j + 1].to_broadcast([P, P]), ident_f[:])
                nc.scalar.copy(out=scale_all[:, K_PASS * g:K_PASS * (g + 1)].rearrange("m (p j) -> m p j", j=4), in_=ps[:].rearrange("m j p -> m p j"))

        x_grouped = {}
        x_codes = {}

        def x_turn(chunk, place, x_bf16):
            if chunk not in x_grouped:
                grouped = xgp.tile([P, 2, 2 * CHUNK], F32, name="x_grouped", tag="x_grouped", align_bytes=64)
                x_grouped[chunk] = grouped
            words = x_bf16.bitcast(F32)
            ps = tps.tile([P, 2, 2, P], F32, name="x_ps", tag="tp")
            for g in range(2):
                for u in range(2):
                    nc.tensor.transpose(ps[:, g, u, :], words[:, 256 * g + u:256 * (g + 1):2], ident_f[:])
            nc.scalar.copy(out=x_grouped[chunk][:, :, place * 256:(place + 1) * 256].rearrange("p g (r u) -> p g r u", u=2),
                           in_=ps[:].rearrange("p g u r -> p g r u"))

        def x_quantise(chunk):
            codes = xcp.tile([P, 2, CHUNK], U32, name="x_codes%d" % chunk, tag="x_codes%d" % chunk, align_bytes=64)
            scales = xcp.tile([P, 2, CHUNK], U8, name="x_scales%d" % chunk, tag="x_scales%d" % chunk, align_bytes=64)
            nc.vector.quantize_mx(out=codes[:].rearrange("p g c -> p (g c)").bitcast(FP8X4), scales=scales[:].rearrange("p g c -> p (g c)"),
                                  in_=x_grouped[chunk][:].rearrange("p g w -> p (g w)").bitcast(BF16))
            x_codes[chunk] = (codes, scales)

        def x1_block(blk):
            b, i = blk // 3, blk % 3
            x_bf16 = xbp.tile([P, D], BF16, name="x_bf16", tag="x_bf16", align_bytes=64)
            for first, width in ((0, K_PASS), (K_PASS, K_PASS)) if blk == 0 else ((0, D),):
                nc.vector.tensor_tensor(out=x_bf16[:, first:first + width], in0=x1_bytes_sb[b][:, i * D + first:i * D + first + width].bitcast(FP8),
                                        in1=scale_all[:, first:first + width], op=ALU.mult)
            x_turn(blk // 4, blk % 4, x_bf16[:])

        groups = [(w, hp) for w in W_ORDER[:2] for hp in range(H // 2)] + [(w, hp) for hp in range(H // 2) for w in W_ORDER[2:]]
        w_grouped = {}
        w_codes = {}

        def w_piece(j, on_gpsimd=False):
            gi, g = j // 2, j % 2
            w, hp = groups[gi]
            if g == 0:
                grouped = wgp.tile([P, 2, 4 * PAIR], BF16, name="w_grouped", tag="w_grouped", align_bytes=64)
                w_grouped[gi] = grouped
            to = w_grouped[gi][:, g, :].rearrange("p (e m r) -> p e m r", e=2, r=4)
            rows = w_raw[(w, g)][:, :, hp * PAIR:(hp + 1) * PAIR].rearrange("p r (m e) -> p e m r", e=2)
            if on_gpsimd:
                nc.gpsimd.tensor_scalar(out=to, in0=rows, scalar1=1.0, scalar2=0.0, op0=ALU.mult, op1=ALU.add)
            else:
                nc.scalar.copy(out=to, in_=rows)

        def w_quantise(gi):
            codes = wcp.tile([P, 2, PAIR], U32, name="w_codes", tag="w_codes", align_bytes=64)
            scales = wcp.tile([P, 2, PAIR], U8, name="w_scales", tag="w_scales", align_bytes=64)
            nc.vector.quantize_mx(out=codes[:].rearrange("p g c -> p (g c)").bitcast(FP8X4), scales=scales[:].rearrange("p g c -> p (g c)"),
                                  in_=w_grouped[gi][:].rearrange("p g c -> p (g c)"))
            w_codes[gi] = (codes, scales)

        def w_quantise_slot(gi):
            return max(2 * gi - 3, gi)

        units = [(gi, chunk) for gi in range(len(groups)) for chunk in ((X2_CHUNK,) if groups[gi][0] >= 2 else (0, 1, 2))]
        last = len(units) - 1
        banks = {}
        products = {}
        turned = {}
        out_sb = {}

        def passes(k, e):
            gi, chunk = units[k]
            wc, ws = w_codes[gi]
            xc, xs = x_codes[chunk]
            bank = accp.tile([P, CHUNK], F32, name="bank%d" % e, tag="bank%d" % e)
            for g in range(2):
                nc.tensor.matmul_mx(out=bank[:], lhsT=wc[:, g, e * P:(e + 1) * P].bitcast(FP8X4), lhsT_scale=ws[:, g, e * P:(e + 1) * P],
                                    rhs=xc[:, g, :].bitcast(FP8X4), rhs_scale=xs[:, g, :], start=(g == 0), stop=(g == 1))
            banks[(k, e)] = bank

        def product(k, e, first=0, width=CHUNK):
            gi, chunk = units[k]
            w, hp = groups[gi]
            at = 6 * P if chunk == X2_CHUNK else P * chunk
            u = up.tile([P, 2, width], F32, name="products%d" % e, tag="products%d" % e)
            nc.vector.scalar_tensor_tensor(out=u[:], in0=banks[(k, e)][:, first:first + width].unsqueeze(1).to_broadcast([P, 2, width]),
                                           scalar=bias_col[:, e, 4 * w + hp:4 * w + hp + 1],
                                           in1=tables[:, 2 * e:2 * e + 2, at + first:at + first + width], op0=ALU.add, op1=ALU.mult)
            for half in range(2):
                if first <= half * 2 * P < first + width:
                    products[(k, e, half)] = u[:, :, half * 2 * P - first:(half + 1) * 2 * P - first]
            products[(k, e)] = u

        def gpsimd_adds_both(k):
            return k % 2 == 1 and 5 <= k < last - 2

        def add_sums(k):
            q0 = 0 if gpsimd_adds_both(k) else 1
            nc.gpsimd.tensor_tensor(out=products[(k, 1)][:, q0:2, :], in0=products[(k, 1)][:, q0:2, :], in1=products[(k, 0)][:, q0:2, :], op=ALU.add)

        def turn(k, half):
            ps = tps.tile([P, 2, 2, P], F32, name="turned", tag="tp")
            for ib in range(2):
                cols = slice(ib * P, (ib + 1) * P)
                for q in range(2):
                    if (q == 0 and not gpsimd_adds_both(k)) or k >= last - 1:
                        nc.tensor.matmul(out=ps[:, q, ib, :], lhsT=products[(k, 0, half)][:, q, cols], rhs=ident_f[:], is_transpose=True, start=True, stop=False)
                        nc.tensor.matmul(out=ps[:, q, ib, :], lhsT=products[(k, 1, half)][:, q, cols], rhs=ident_f[:], is_transpose=True, start=False, stop=True)
                    else:
                        nc.tensor.transpose(ps[:, q, ib, :], products[(k, 1, half)][:, q, cols], ident_f[:])
            turned[(k, half)] = ps

        def empty(to, bank, factor):
            if factor == 1.0:
                nc.scalar.copy(out=to, in_=bank)
            else:
                nc.scalar.activation(out=to, in_=bank, func=ACT.Copy, scale=factor)

        def leave(k, half):
            gi, chunk = units[k]
            w, hp = groups[gi]
            factor = Q_FACTOR if w % 2 == 0 else 1.0
            if chunk == X2_CHUNK:
                if half == 0:
                    o2 = op.tile([P, B, 2, DH], F32, name="out2_sb", tag="out2_sb", bufs=4)
                    out_sb[0] = o2
                empty(out_sb[0][:, 2 * half:2 * half + 2, :, :].rearrange("p b hh (j e) -> p (b hh j) e", e=2),
                      turned[(k, half)][:].rearrange("p e b x -> p (b x) e"), factor)
                if k == last:
                    for b in (2 * half, 2 * half + 1):
                        nc.sync.dma_start(out=outs[w][b, 2 * hp:2 * hp + 2, N1:N1 + N2, :].rearrange("hh p c -> p hh c"), in_=out_sb[0][:, b, :, :])
                elif half == 1:
                    for hh in range(2):
                        nc.sync.dma_start(out=outs[w][:, 2 * hp + hh, N1:N1 + N2, :].rearrange("b p c -> p b c"), in_=out_sb[0][:, :, hh, :])
                return
            for ib in range(2):
                blk = 2 * half + ib
                b, i = (4 * chunk + blk) // 3, (4 * chunk + blk) % 3
                if i == 0:
                    o1 = op.tile([P, 2, 3, DH], F32, name="out1_sb", tag="out1_sb", bufs=6)
                    out_sb[b] = o1
                empty(out_sb[b][:, :, i, :].rearrange("p hh (j e) -> p hh j e", e=2),
                      turned[(k, half)][:, :, ib, :].rearrange("p e (hh j) -> p hh j e", hh=2), factor)
                if i == 2:
                    nc.sync.dma_start(out=outs[w][b, 2 * hp:2 * hp + 2, 0:N1, :].rearrange("hh (p i) c -> p hh (i c)", i=3),
                                      in_=out_sb[b][:].rearrange("p hh i c -> p hh (i c)"))

        def keep_clock_up(blk):
            idle = accp.tile([P, CHUNK], F32, name="idle", tag="bank%d" % (blk % 2))
            for again in range(2):
                nc.tensor.matmul(out=idle[:], lhsT=ident_b[:], rhs=zeros[:], start=True, stop=True)

        spread_scales()
        table2_turn()
        for t in range(4):
            table_leave(t, 2)
        for blk in range(BLOCKS_1):
            if blk == BLOCKS_1 - 2:
                passes(0, 0)
                passes(0, 1)
            if blk < BLOCKS_1 - 2:
                keep_clock_up(blk)
            x1_block(blk)
            if blk == 8:
                constants()
            if 2 <= blk < 10:
                table_leave((blk - 2) // 2, (blk - 2) % 2)
            if blk in (3, 5):
                w_piece((blk - 3) // 2)
            if blk in (1, 3, 5, 7):
                table_turn(blk // 2)
            if blk in (5, 10):
                x_quantise((blk - 5) // 5)
            if blk == BLOCKS_1 - 3:
                w_quantise(0)

        for n in range(-PIECE_LEAD, len(units) + BEHIND):
            live = 0 <= n <= last
            ahead = 1 <= n + AHEAD <= last
            behind = 0 <= n - BEHIND <= last
            if behind:
                turn(n - BEHIND, 0)
                turn(n - BEHIND, 1)
            if n in TURN_FREE_SLOTS:
                for b in (2 * n, 2 * n + 1):
                    x_turn(X2_CHUNK, b, x2_sb[:, b, :])
            if live and n < last:
                product(n, 1)
                product(n, 0)
            if n == last:
                for half in range(2):
                    product(n, 1, half * 2 * P, 2 * P)
                    product(n, 0, half * 2 * P, 2 * P)
            for gi in range(1, len(groups)):
                if n == w_quantise_slot(gi):
                    w_quantise(gi)
            if n == 0:
                x_quantise(2)
            if n == X2_QUANTISE_SLOT:
                x_quantise(X2_CHUNK)
            if live and n < last - 1:
                add_sums(n)
            if ahead:
                passes(n + AHEAD, 0)
                passes(n + AHEAD, 1)
            if behind:
                leave(n - BEHIND, 0)
            if 2 <= n + PIECE_LEAD < 2 * len(groups):
                w_piece(n + PIECE_LEAD, on_gpsimd=n == 0)
            if n == 3:
                load_w(W_ORDER[3])
            if behind:
                leave(n - BEHIND, 1)
